import numpy as np
import ml_dtypes


def mxq(x, axis, fmt="e4m3"):
    dtype, down = {"e4m3": (ml_dtypes.float8_e4m3fn, 7), "e5m2": (ml_dtypes.float8_e5m2, 14)}[fmt]
    v = np.moveaxis(np.asarray(x, np.float32).astype(ml_dtypes.bfloat16).astype(np.float64), axis, -1)
    blocks = v.reshape(v.shape[:-1] + (-1, 32))
    amax = np.abs(blocks).max(-1, keepdims=True)
    byte = np.maximum(np.where(amax > 0, np.frexp(amax)[1] - 1 + 127, 0) - down, 1)
    scale = np.exp2(byte - 127.0)
    codes = (blocks / scale).astype(np.float32).astype(dtype).astype(np.float64)
    return np.moveaxis((codes * scale).reshape(v.shape), -1, axis)


WIDE = False


def mx_kscale(k):
    if not WIDE:
        return np.ones(k)
    levels = np.array([10, -10, 5, -5, 0])
    if k % 512:
        return np.exp2(np.random.permutation(np.resize(levels, k // 32))).repeat(32)
    a = np.empty((k // 512, 16))
    for p in range(k // 512):
        a[p, :8] = np.random.permutation(np.resize(levels, 8))
        for g in range(8):
            far = levels[np.abs(levels - a[p, g]) >= 10]
            a[p, g + 8] = far[np.random.randint(len(far))]
    return np.exp2(a.ravel()).repeat(32)


BF16 = ml_dtypes.bfloat16


def bf(x):
    return np.asarray(x, np.float32).astype(BF16)


def f64(x):
    return np.asarray(x).astype(np.float64)


E2M1 = np.array([0.0, 0.5, 1.0, 1.5, 2.0, 3.0, 4.0, 6.0, -0.0, -0.5, -1.0, -1.5, -2.0, -3.0, -4.0, -6.0])


def pack_weight(w, fmt):
    k, n = w.shape
    w = f64(bf(w)).reshape(k // 32, 32, n)
    amax = np.abs(w).max(1)
    if fmt == "e4m3":
        byte = np.frexp(amax)[1] - 1 + 127 - 7
    else:
        mant, ex = np.frexp(amax / 6.0)
        byte = np.where(mant > 0.5, ex, ex - 1) + 127
    byte = np.clip(np.where(amax > 0, byte, 1), 1, 254)
    scaled = (w * np.exp2(127.0 - byte)[:, None, :]).reshape(k, n).astype(np.float32)
    by_word = np.ascontiguousarray(scaled.reshape(k // 512, 128, 4, n).transpose(0, 1, 3, 2))
    if fmt == "e4m3":
        words = by_word.astype(ml_dtypes.float8_e4m3fn).view(np.uint8)
    else:
        c = by_word.astype(ml_dtypes.float4_e2m1fn).view(np.uint8) & 0xF
        words = c[..., 0::2] | (c[..., 1::2] << 4)
    return np.ascontiguousarray(words), np.ascontiguousarray(byte.astype(np.uint8).reshape(k // 512, 16, n))


def unpack_weight(words, scales, fmt):
    g, p, n, _ = words.shape
    if fmt == "e4m3":
        vals = np.ascontiguousarray(words).view(ml_dtypes.float8_e4m3fn).astype(np.float64)
    else:
        nib = np.empty((g, p, n, 4), np.uint8)
        nib[..., 0::2] = words & 0xF
        nib[..., 1::2] = words >> 4
        vals = E2M1[nib]
    vals = vals * np.repeat(np.exp2(scales.astype(np.float64) - 127.0), 8, axis=1)[..., None]
    return vals.transpose(0, 1, 3, 2).reshape(g * 512, n)


B, N, F, C0, C1, E, G = 2, 512, 2048, 2048, 1024, 2, 4
EPS_BN = 1e-5
SLOPE = 0.01
R = B * N
CG = (E + 1) * F // G
OG = C0 // G


def bn_train(y, gamma, beta):
    mean = y.mean(axis=(0, 1), keepdims=True)
    var = y.var(axis=(0, 1), keepdims=True)
    return (y - mean) / np.sqrt(var + EPS_BN) * gamma + beta


def leaky(v):
    return np.where(v >= 0.0, v, SLOPE * v)


def draw0():
    s = mx_kscale(CG)
    sx = np.tile(s, G)
    t = mx_kscale(C0)
    node_feat = bf(np.random.standard_normal((B, N, F)) * 5.0 * sx[:F])
    aggr = bf(np.random.standard_normal((B, N, E * F)) * 6.0 / np.sqrt(N) * sx[F:])
    w0_words, w0_scales = pack_weight((np.random.standard_normal((C0, CG)) / np.sqrt(CG) / s).T, "e4m3")
    gamma0 = bf((1.0 + 0.1 * np.random.standard_normal(C0)) * t)
    beta0 = bf(0.1 * np.random.standard_normal(C0) * t)
    w1_words, w1_scales = pack_weight((np.random.standard_normal((C1, C0)) / np.sqrt(C0) / t).T, "e4m3")
    return {"node_feat": node_feat,
            "aggr": aggr,
            "w0_words": w0_words,
            "w0_scales": w0_scales,
            "gamma0": gamma0,
            "beta0": beta0,
            "w1_words": w1_words,
            "w1_scales": w1_scales,
            "gamma1": bf(1.0 + 0.1 * np.random.standard_normal(C1)),
            "beta1": bf(0.1 * np.random.standard_normal(C1))}


def core(node_feat, aggr, w0_words, w0_scales, gamma0, beta0, w1_words, w1_scales, gamma1, beta1):
    x = np.concatenate([f64(node_feat), f64(aggr)], axis=-1)
    xg = x.reshape(R, G, CG).transpose(1, 0, 2)
    wg = unpack_weight(w0_words, w0_scales, "e4m3").T.reshape(G, OG, CG).transpose(0, 2, 1)
    y0 = mxq(xg, 2, "e4m3") @ wg
    y0 = y0.transpose(1, 0, 2).reshape(B, N, C0)
    h = leaky(bn_train(y0, f64(gamma0), f64(beta0)))
    y1 = (mxq(h.reshape(R, C0), 1, "e4m3") @ unpack_weight(w1_words, w1_scales, "e4m3")).reshape(B, N, C1)
    return leaky(bn_train(y1, f64(gamma1), f64(beta1)))


def e4m3fn_bytes(y):
    return np.clip(np.asarray(y, np.float64), -448.0, 448.0).astype(np.float32).astype(ml_dtypes.float8_e4m3fn).view(np.uint8)


def e4m3fn_values(b):
    return np.asarray(b, np.uint8).view(ml_dtypes.float8_e4m3fn).astype(np.float64)


def setup_inputs():
    d = draw0()
    x0 = np.asarray(d['aggr']).astype(np.float64)
    s = (np.max(np.abs(x0), axis=(0, 1), keepdims=True) / 448.0).astype(np.float32)
    out = {}
    for k, v in d.items():
        if k == 'aggr':
            out['aggr_bytes'] = e4m3fn_bytes(x0 / s.astype(np.float64))
            out['aggr_scale'] = s
        else:
            out[k] = v
    return out


def reference(node_feat, aggr_bytes, aggr_scale, w0_words, w0_scales, gamma0, beta0, w1_words, w1_scales, gamma1, beta1):
    return core(node_feat, e4m3fn_values(aggr_bytes) * aggr_scale.astype(np.float64), w0_words, w0_scales, gamma0, beta0, w1_words, w1_scales, gamma1, beta1)

@@ -1,0 +1,510 @@
+from contextlib import ExitStack
+
+import concourse.mybir as mybir
+from concourse.masks import make_identity
+
+R, C0, C1 = 1024, 2048, 1024
+F, EF = 2048, 4096
+G, CG, OG = 4, 1536, 512
+EPS = 1e-5
+SLOPE = 0.01
+FLOPS = 2 * R * CG * C0 + 2 * R * C0 * C1
+
+P = 128
+KC = 512
+NB = R // P
+HALF = 512
+
+F32 = mybir.dt.float32
+BF16 = mybir.dt.bfloat16
+U32 = mybir.dt.uint32
+I32 = mybir.dt.int32
+U8 = mybir.dt.uint8
+FP8 = mybir.dt.float8_e4m3fn
+FP8X4 = mybir.dt.float8_e4m3fn_x4
+ALU = mybir.AluOpType
+ACT = mybir.ActivationFunctionType
+
+VSTATS = {(0, 1), (3, 0), (3, 1)}
+CONV = [2, 2, 2]
+SOP = [9,4,4]
+LOFF = [5,5,14]
+QOFF = 2
+HEAD = ["a1a","a1b","n2","n0b","n0a","n1","w","a2a","a2b","ws","n3"]
+PERM = [5,4,4,4]
+SPREAD = [2,4,1,12,13,19]
+G3 = 10
+RATE = [14,24,38,64,64]
+
+
+def tile_nodeupdatenetwork_pb_w8_kernel(
+    tc, node_feat, aggr_bytes, aggr_scale, w0_words, w0_scales, gamma0, beta0, w1_words, w1_scales, gamma1, beta1, out
+):
+    nc = tc.nc
+    node_v = node_feat.flatten_outer_dims().rearrange("(b p) k -> p b k", p=P)
+    aggr_v = aggr_bytes.flatten_outer_dims().rearrange("(b p) k -> p b k", p=P)
+    scale_v = aggr_scale.rearrange("a b k -> (a b k)")
+    w0_v = w0_words.bitcast(I32).rearrange("g p n o -> p g (n o)")
+    w1_v = w1_words.bitcast(I32).rearrange("g p n o -> p g (n o)")
+    out_v = out.flatten_outer_dims().rearrange("(b p) c -> p b c", p=P)
+
+    with ExitStack() as ctx:
+        keep = ctx.enter_context(tc.tile_pool(name="keep", bufs=1))
+        work = ctx.enter_context(tc.tile_pool(name="work", bufs=2))
+        psum = ctx.enter_context(tc.psum_pool(name="psum", bufs=4))
+
+        def wt(shape, dtype, tag, bufs):
+            return work.tile(shape, dtype, name=tag, tag=tag, bufs=bufs, align_bytes=64)
+
+        ctx.enter_context(tc.manual_schedule())
+        w0s_raw = keep.tile([P, C0], U8, name="w0s_raw", align_bytes=64)
+        w1s = keep.tile([P, C1], U8, name="w1s", align_bytes=64)
+        nc.vector.memset(w0s_raw[:].bitcast(I32), 0)
+        nc.vector.memset(w1s[:].bitcast(I32), 0)
+        ident = keep.tile([P, P], F32, name="ident", align_bytes=64)
+        make_identity(nc, ident[:])
+        neghalf = keep.tile([P, 4], F32, name="neghalf", align_bytes=64)
+        nc.gpsimd.memset(neghalf[:], -0.5)
+        gb1_rows = keep.tile([P, P], BF16, name="gb1_rows", align_bytes=64)
+        nc.gpsimd.memset(gb1_rows[:], 0.0)
+        g0b = keep.tile([P, G, 4], BF16, name="g0b", align_bytes=64)
+        b0b = keep.tile([P, G, 4], BF16, name="b0b", align_bytes=64)
+        nc.scalar.dma_start(out=g0b[:], in_=gamma0.rearrange("(g p t) -> p g t", p=P, t=4))
+        nc.scalar.dma_start(out=b0b[:], in_=beta0.rearrange("(g p t) -> p g t", p=P, t=4))
+        nc.scalar.dma_start(out=gb1_rows[0:8, :], in_=gamma1.rearrange("(c p) -> c p", p=P))
+        nc.scalar.dma_start(out=gb1_rows[8:16, :], in_=beta1.rearrange("(c p) -> c p", p=P))
+
+        xb = {}
+        ab = {}
+        sc = {}
+        w0raw = {}
+
+        def chunk_tile(c):
+            xb[c] = wt([P, NB, KC], BF16, "xb", 6)
+
+        def load_node(c, b0, b1):
+            nc.sync.dma_start(out=xb[c][:, b0:b1, :], in_=node_v[:, b0:b1, c * KC : (c + 1) * KC])
+
+        def aggr_cols(g):
+            lo = max(0, g * CG - F)
+            return lo, (g + 1) * CG - F
+
+        def aggr_tiles(g):
+            lo, hi = aggr_cols(g)
+            ab[g] = wt([P, NB, hi - lo], U8, "ab", 2)
+            sc[g] = wt([P, hi - lo], F32, "sc", 2)
+
+        def load_aggr(g, b0, b1):
+            lo, hi = aggr_cols(g)
+            nc.sync.dma_start(out=ab[g][:, b0:b1, :], in_=aggr_v[:, b0:b1, lo:hi])
+
+        scale_rows = keep.tile([P, P], F32, name="scale_rows", align_bytes=64)
+        nc.vector.memset(scale_rows[:], 0.0)
+        nc.sync.dma_start(out=scale_rows[0 : EF // P, :], in_=scale_v.rearrange("(m n) -> m n", n=P))
+        scale_cols = keep.tile([P, EF // P], F32, name="scale_cols", align_bytes=64)
+
+        def spread_scale(c):
+            g = c // 3
+            lo = c * KC - F
+            pt = psum.tile([P, 4, P], F32, name="pt", tag="pt", bufs=4)
+            for q in range(4):
+                m = lo // P + q
+                nc.tensor.transpose(pt[:, q, :], scale_cols[:, m : m + 1].to_broadcast([P, P]), ident[:])
+            rel = lo - aggr_cols(g)[0]
+            nc.scalar.copy(out=sc[g][:, rel : rel + KC], in_=pt[:].rearrange("p q n -> p (q n)"))
+
+
+        def load_w0(g):
+            w0raw[g] = wt([P, 3, OG], I32, "w0raw", 1)
+            nc.sync.dma_start(out=w0raw[g][:], in_=w0_v[:, :, g * OG : (g + 1) * OG])
+
+        def load_plane(tile, scales, passes):
+            sv = scales.bitcast(I32)
+            for q in range(4):
+                nc.sync.dma_start(out=tile[32 * q : 32 * q + 4 * passes, :].bitcast(I32), in_=sv[:, 4 * q : 4 * q + 4, :])
+
+        aggr_tiles(1)
+        for c in range(4):
+            chunk_tile(c)
+        aggr_tiles(2)
+        loads = {
+            "a1a": (load_aggr, 1, 0, 4), "a1b": (load_aggr, 1, 4, 8),
+            "n0a": (load_node, 0, 0, 4), "n0b": (load_node, 0, 4, 8), "n1": (load_node, 1, 0, 8), "n2": (load_node, 2, 0, 8), "n3": (load_node, 3, 0, 8),
+            "a2a": (load_aggr, 2, 0, 4), "a2b": (load_aggr, 2, 4, 8), "w": (load_w0, 0), "ws": (load_plane, w0s_raw, w0_scales, 3),
+        }
+        for name in HEAD:
+            fn, *args = loads[name]
+            fn(*args)
+
+        pieces = [(c, b) for c in range(4, 12) for b in range(NB)]
+        pos = [0]
+
+        def fill(upto):
+            for c, b in pieces[pos[0] : upto]:
+                if b == 0:
+                    chunk_tile(c)
+                g = c // 3
+                lo = c * KC - F - aggr_cols(g)[0]
+                nc.vector.tensor_tensor(
+                    out=xb[c][:, b, :],
+                    in0=ab[g][:, b, lo : lo + KC].bitcast(FP8),
+                    in1=sc[g][:, lo : lo + KC],
+                    op=ALU.mult,
+                )
+            pos[0] = max(pos[0], min(upto, len(pieces)))
+
+        xg = {}
+
+        pts = {}
+
+        def turn(s):
+            c, bank = s // 4, s % 4
+            words = xb[c][:].rearrange("p b k -> p (b k)").bitcast(F32)
+            pt = psum.tile([P, 2, 2, P], F32, name="pt", tag="pt", bufs=4)
+            for q in range(2):
+                b = 2 * bank + q
+                for u in range(2):
+                    nc.tensor.transpose(pt[:, q, u, :], words[:, 256 * b + u : 256 * (b + 1) : 2], ident[:])
+            pts[s] = pt
+
+        def empty(s):
+            c, bank = s // 4, s % 4
+            if bank == 0:
+                xg[c] = wt([P, R * 4], BF16, "xg", 2)
+            dst = xg[c][:].bitcast(F32).rearrange("p (b r u) -> p b r u", r=P, u=2)
+            nc.scalar.copy(out=dst[:, 2 * bank : 2 * bank + 2], in_=pts[s][:].rearrange("p q u r -> p q r u"))
+
+        xq = {}
+        xs = {}
+
+        def quant(c):
+            xq[c] = wt([P, R], U32, "xq", 6)
+            xs[c] = wt([P, R], U8, "xs", 6)
+            nc.vector.quantize_mx(out=xq[c][:].bitcast(FP8X4), scales=xs[c][:], in_=xg[c][:])
+
+        w0p = {}
+        w0s = {}
+
+        def permute(g):
+            w0p[g] = wt([P, 3, OG], I32, "w0p", 2)
+            w0s[g] = wt([P, OG], U8, "w0s", 2)
+            for j in range(3):
+                nc.vector.tensor_copy(
+                    out=w0p[g][:, j, :].rearrange("p (t m) -> p m t", t=4),
+                    in_=w0raw[g][:, j, :].rearrange("p (m t) -> p m t", t=4),
+                )
+            nc.vector.tensor_copy(
+                out=w0s[g][:].rearrange("p (t m) -> p m t", t=4),
+                in_=w0s_raw[:, g * OG : (g + 1) * OG].rearrange("p (m t) -> p m t", t=4),
+            )
+
+        def coefficients(var, factor, mean, sign, gamma, beta, n, tag):
+            ve = wt([P, n], F32, tag + "ve", 2)
+            a = wt([P, n], F32, tag + "a", 4)
+            m = wt([P, n], F32, tag + "m", 2)
+            b = wt([P, n], F32, tag + "b", 4)
+            nc.gpsimd.tensor_scalar(out=ve[:], in0=var, scalar1=factor, scalar2=EPS, op0=ALU.mult, op1=ALU.add)
+            nc.gpsimd.tensor_tensor(out=ve[:], in0=ve[:], in1=neghalf[:, 0:n], op=ALU.pow)
+            nc.gpsimd.tensor_tensor(out=a[:], in0=ve[:], in1=gamma, op=ALU.mult)
+            nc.gpsimd.tensor_tensor(out=m[:], in0=mean, in1=a[:], op=ALU.mult)
+            nc.gpsimd.tensor_tensor(out=b[:], in0=beta, in1=m[:], op=sign)
+            return a, b
+
+        def bn_tile(halves, mv, i):
+            bs = wt([P, 2, 6], F32, "bs", 3)
+            for h in range(2):
+                nc.vector.bn_stats(out=bs[:, h, :], in_=halves[h][:])
+            nc.vector.bn_aggr(out=mv[:, i, :], in_=bs[:].rearrange("p h s -> p (h s)"))
+
+        def bn_coefficients(mv, gamma, beta, n, tag):
+            return coefficients(mv[:, :, 1], 1.0, mv[:, :, 0], ALU.subtract, gamma, beta, n, tag)
+
+        y = {}
+        v = {}
+        coef = {}
+        part = {}
+
+        def conv0(g, t, tag="acc"):
+            y[g, t] = []
+            for h in range(2):
+                acc = psum.tile([P, HALF], F32, name=tag, tag=tag, bufs=4)
+                for j in range(3):
+                    c = 3 * g + j
+                    nc.tensor.matmul_mx(
+                        out=acc[:],
+                        lhsT=w0p[g][:, j, P * t : P * (t + 1)].bitcast(FP8X4),
+                        lhsT_scale=w0s[g][4 * j : P, P * t : P * (t + 1)],
+                        rhs=xq[c][:, HALF * h : HALF * (h + 1)].bitcast(FP8X4),
+                        rhs_scale=xs[c][:, HALF * h : HALF * (h + 1)],
+                        start=(j == 0),
+                        stop=(j == 2),
+                    )
+                y[g, t].append(acc)
+
+        def v_tile(g):
+            if g not in v:
+                v[g] = wt([P, 4, R], F32, "v", 2)
+
+        def gb0(g, pair):
+            return g0f[:, g, 2 * pair : 2 * pair + 2], b0f[:, g, 2 * pair : 2 * pair + 2]
+
+        def bn0(g, t):
+            pair, i = t // 2, t % 2
+            if i == 0:
+                part[g, pair] = wt([P, 2, 2], F32, "mv", 3)
+            bn_tile(y[g, t], part[g, pair], i)
+            if i == 1:
+                gamma, beta = gb0(g, pair)
+                coef[g, pair] = bn_coefficients(part[g, pair], gamma, beta, 2, "c")
+
+        def apply_psum(g, t, halves=(0, 1)):
+            v_tile(g)
+            a, b = coef[g, t // 2]
+            i = t % 2
+            for h in halves:
+                nc.scalar.activation(
+                    out=v[g][:, t, HALF * h : HALF * (h + 1)],
+                    in_=y[g, t][h][:],
+                    func=ACT.Identity,
+                    bias=b[:, i : i + 1],
+                    scale=a[:, i : i + 1],
+                )
+
+        def sum0(g, t):
+            v_tile(g)
+            pair, i = t // 2, t % 2
+            if i == 0:
+                part[g, pair] = wt([P, 2, 2], F32, "sm", 3)
+            sm = part[g, pair]
+            for h in range(2):
+                nc.scalar.activation(
+                    out=v[g][:, t, HALF * h : HALF * (h + 1)],
+                    in_=y[g, t][h][:],
+                    func=ACT.Copy,
+                    accum_out=sm[:, i, h : h + 1],
+                )
+            if i == 1:
+                tot = wt([P, 2], F32, "tot", 2)
+                nm = wt([P, 2], F32, "nm", 3)
+                nc.gpsimd.tensor_tensor(out=tot[:], in0=sm[:, :, 0], in1=sm[:, :, 1], op=ALU.add)
+                nc.gpsimd.tensor_scalar(
+                    out=nm[:], in0=tot[:], scalar1=-1.0 / R, scalar2=0.0, op0=ALU.mult, op1=ALU.add
+                )
+                part[g, pair] = (nm, wt([P, 2], F32, "sq", 3))
+
+        def square0(g, t):
+            pair, i = t // 2, t % 2
+            nm, sq = part[g, pair]
+            junk = wt([P, R], BF16, "junk", 1)
+            nc.scalar.activation(
+                out=junk[:], in_=v[g][:, t, :], func=ACT.Square, bias=nm[:, i : i + 1], accum_out=sq[:, i : i + 1]
+            )
+            if i == 1:
+                gamma, beta = gb0(g, pair)
+                coef[g, pair] = coefficients(sq[:], 1.0 / R, nm[:], ALU.add, gamma, beta, 2, "c")
+
+        def apply_sbuf(g, t):
+            a, b = coef[g, t // 2]
+            i = t % 2
+            nc.scalar.activation(
+                out=v[g][:, t, :], in_=v[g][:, t, :], func=ACT.Identity, bias=b[:, i : i + 1], scale=a[:, i : i + 1]
+            )
+
+        hg = {}
+        hq = {}
+        hs = {}
+
+        def leaky0(g, h):
+            hg[g, h] = wt([P, HALF, 4], BF16, "hg", 2)
+            vin = v[g][:, :, HALF * h : HALF * (h + 1)].rearrange("p t r -> p r t")
+            nc.vector.scalar_tensor_tensor(out=hg[g, h][:], in0=vin, scalar=SLOPE, in1=vin, op0=ALU.mult, op1=ALU.max)
+
+        def quant_h(g, h):
+            if h == 0:
+                hq[g] = keep.tile([P, R], U32, name="hq%d" % g, align_bytes=64)
+                hs[g] = keep.tile([P, R], U8, name="hs%d" % g, align_bytes=64)
+            nc.vector.quantize_mx(
+                out=hq[g][:, HALF * h : HALF * (h + 1)].bitcast(FP8X4),
+                scales=hs[g][:, HALF * h : HALF * (h + 1)],
+                in_=hg[g, h][:].rearrange("p r t -> p (r t)"),
+            )
+
+        y2 = {}
+
+        def conv1(ct, h, passes):
+            if ct not in y2:
+                tag = "acc" if ct in (0, 1, 4, 7) else "pt"
+                y2[ct] = [psum.tile([P, HALF], F32, name=tag, tag=tag, bufs=4) for i in range(2)]
+            for g in passes:
+                nc.tensor.matmul_mx(
+                    out=y2[ct][h][:],
+                    lhsT=w1[:, g, P * ct : P * (ct + 1)].bitcast(FP8X4),
+                    lhsT_scale=w1s[4 * g : P, P * ct : P * (ct + 1)],
+                    rhs=hq[g][:, HALF * h : HALF * (h + 1)].bitcast(FP8X4),
+                    rhs_scale=hs[g][:, HALF * h : HALF * (h + 1)],
+                    start=(g == 0),
+                    stop=(g == 3),
+                )
+
+        v2 = {}
+        w2 = {}
+        coef2 = {}
+
+        def norm1(ct):
+            mv = wt([P, 1, 2], F32, "mv1", 3)
+            bn_tile(y2[ct], mv, 0)
+            coef2[ct] = bn_coefficients(mv, gb1[:, ct : ct + 1], gb1[:, 8 + ct : 9 + ct], 1, "d")
+
+        def apply1(ct):
+            v2[ct] = wt([P, R], F32, "xg", 2)
+            w2[ct] = wt([P, R], F32, "xq", 6)
+            a, b = coef2[ct]
+            for h in range(2):
+                cols = slice(HALF * h, HALF * (h + 1))
+                nc.scalar.activation(
+                    out=v2[ct][:, cols], in_=y2[ct][h][:], func=ACT.Identity, bias=b[:, 0:1], scale=a[:, 0:1]
+                )
+                nc.vector.scalar_tensor_tensor(
+                    out=w2[ct][:, cols], in0=v2[ct][:, cols], scalar=SLOPE, in1=v2[ct][:, cols], op0=ALU.mult, op1=ALU.max
+                )
+
+        o = {}
+
+        def store(ct):
+            if ct % 2 == 0:
+                o[ct // 2] = wt([P, NB, 2 * P], F32, "xb", 6)
+            ob = o[ct // 2]
+            lo = P * (ct % 2)
+            for h in range(2):
+                ot = psum.tile([P, 4, P], F32, name="acc", tag="acc", bufs=4)
+                for q in range(4):
+                    b = 4 * h + q
+                    nc.tensor.transpose(ot[:, q, :], w2[ct][:, P * b : P * (b + 1)], ident[:])
+                nc.scalar.copy(out=ob[:, 4 * h : 4 * h + 4, lo : lo + P], in_=ot[:])
+                if ct % 2 == 1:
+                    nc.sync.dma_start(
+                        out=out_v[:, 4 * h : 4 * h + 4, P * (ct - 1) : P * (ct + 1)], in_=ob[:, 4 * h : 4 * h + 4, :]
+                    )
+
+        g0f = keep.tile([P, G, 4], F32, name="g0f", align_bytes=64)
+        b0f = keep.tile([P, G, 4], F32, name="b0f", align_bytes=64)
+        nc.gpsimd.tensor_copy(out=g0f[:], in_=g0b[:])
+        nc.gpsimd.tensor_copy(out=b0f[:], in_=b0b[:])
+        gb1_f = keep.tile([P, P], F32, name="gb1_f", align_bytes=64)
+        nc.gpsimd.tensor_copy(out=gb1_f[:], in_=gb1_rows[:])
+        gb1 = keep.tile([P, 16], F32, name="gb1", align_bytes=64)
+        w1 = keep.tile([P, 4, C1], I32, name="w1", align_bytes=64)
+
+        steps = {}
+
+        def at(step, fn, *args):
+            steps.setdefault(step, []).append((fn, args))
+
+        for c in range(12):
+            if c < 11:
+                at(4 * c + 3 + QOFF, quant, c)
+        for g in range(G):
+            base = 12 * (g + 1)
+            at(base - PERM[g], permute, g)
+            if g < 3:
+                at(base - 1, load_w0, g + 1)
+                on_vector = tuple((g, p) in VSTATS for p in range(2))
+                s = base + SOP[g]
+                at(s - 1, conv0, g, 0)
+                at(s, conv0, g, 1)
+                if on_vector == (True, True):
+                    plan = [(0, bn0, 0), (1, bn0, 1), (3, apply_psum, 0), (4, apply_psum, 1), (4, conv0, 2), (5, conv0, 3)]
+                    plan += [(5, bn0, 2), (6, bn0, 3), (8, apply_psum, 2), (9, apply_psum, 3)]
+                elif on_vector == (False, True):
+                    plan = [(0, sum0, 0), (1, sum0, 1), (1, conv0, 2), (2, conv0, 3), (2, bn0, 2), (3, bn0, 3)]
+                    plan += [(2, square0, 0), (3, square0, 1)]
+                    plan += [(5, apply_psum, 2), (6, apply_psum, 3), (7, apply_sbuf, 0), (8, apply_sbuf, 1)]
+                else:
+                    plan = [(0, sum0, 0), (1, sum0, 1), (1, conv0, 2), (2, conv0, 3), (2, sum0, 2), (3, sum0, 3)]
+                    plan += [(4 + t, square0, t) for t in range(4)] + [(8 + t, apply_sbuf, t) for t in range(4)]
+                for k, fn, t in plan:
+                    at(s + k, fn, g, t)
+                s += plan[-1][0]
+                s += LOFF[g]
+                at(s, leaky0, g, 0)
+                at(s + 1, leaky0, g, 1)
+                at(s + 1, quant_h, g, 0)
+                at(s + 2, quant_h, g, 1)
+
+        def load_group3():
+            aggr_tiles(3)
+            load_aggr(3, 0, 8)
+
+        def load_w1():
+            for half in range(2):
+                nc.sync.dma_start(out=w1[:, 2 * half : 2 * half + 2, :], in_=w1_v[:, 2 * half : 2 * half + 2, :])
+            load_plane(w1s, w1_scales, 4)
+
+        def turn_gb1():
+            gpt = psum.tile([P, P], F32, name="pt", tag="pt", bufs=4)
+            nc.tensor.transpose(gpt[:], gb1_f[:], ident[:])
+            nc.scalar.copy(out=gb1[:], in_=gpt[:, 0:16])
+
+        at(G3, load_group3)
+        at(20, load_w1)
+        at(8, turn_gb1)
+
+        spt = psum.tile([P, P], F32, name="pt", tag="pt", bufs=4)
+        nc.tensor.transpose(spt[:], scale_rows[:], ident[:])
+        nc.scalar.copy(out=scale_cols[:], in_=spt[:, 0 : EF // P])
+        spread_scale(4)
+        spread_scale(5)
+        for c in range(6, 12):
+            at(SPREAD[c - 6], spread_scale, c)
+        fill(8)
+        turn(0)
+        turn(1)
+        for s in range(48):
+            if s + 2 < 48:
+                turn(s + 2)
+            empty(s)
+            k = (s + 1) / 12
+            lo = int(k)
+            fill(int(RATE[lo] + (k - lo) * (RATE[min(4, lo + 1)] - RATE[lo])))
+            for fn, args in steps.get(s, []):
+                fn(*args)
+
+        quant(11)
+        for t in range(4):
+            conv0(3, t, "acc" if t < 2 else "pt")
+        for t in range(4):
+            bn0(3, t)
+        for s in range(48, 80):
+            for fn, args in steps.get(s, []):
+                if fn in (square0, apply_psum, apply_sbuf):
+                    fn(*args)
+        for s in range(48, 80):
+            for fn, args in steps.get(s, []):
+                if fn in (leaky0, quant_h):
+                    fn(*args)
+        for h in range(2):
+            for t in range(2):
+                apply_psum(3, t, (h,))
+        for ct in range(2):
+            for h in range(2):
+                conv1(ct, h, range(0, 3))
+        for h in range(2):
+            for t in range(2, 4):
+                apply_psum(3, t, (h,))
+        for ct in range(2, 4):
+            for h in range(2):
+                conv1(ct, h, range(0, 3))
+        leaky0(3, 0)
+        leaky0(3, 1)
+        quant_h(3, 0)
+        quant_h(3, 1)
+
+        for s in range(11):
+            if 0 <= s - 2 < 8:
+                apply1(s - 2)
+            if s < 8:
+                for h in range(2):
+                    conv1(s, h, range(3, 4) if s < 4 else range(0, 4))
+                norm1(s)
+            if 0 <= s - 3 < 8:
+                store(s - 3)

@@ -25,16 +25,16 @@ FP8X4 = mybir.dt.float8_e4m3fn_x4
 ALU = mybir.AluOpType
 ACT = mybir.ActivationFunctionType
 
-VSTATS = {(0, 1), (3, 0), (3, 1)}
+VSTATS = {(0, 1), (1, 1), (3, 0), (3, 1)}
 CONV = [2, 2, 2]
-SOP = [9,4,4]
-LOFF = [5,5,14]
+SOP = [6,4,6]
+LOFF = [12,3,10]
 QOFF = 2
-HEAD = ["a1a","a1b","n2","n0b","n0a","n1","w","a2a","a2b","ws","n3"]
-PERM = [5,4,4,4]
-SPREAD = [2,4,1,12,13,19]
-G3 = 10
-RATE = [14,24,38,64,64]
+HEAD = ["n2","n0a","w","n0b","a1a","n1","a1b","ws","a2a","n3","a2b"]
+PERM = [7,4,3,5]
+SPREAD = [4,5,3,12,15,19]
+G3 = 11
+RATE = [8,20,44,64,64]
 
 
 def tile_nodeupdatenetwork_pb_w8_kernel(
@@ -63,8 +63,8 @@ def tile_nodeupdatenetwork_pb_w8_kernel(
         nc.vector.memset(w1s[:].bitcast(I32), 0)
         ident = keep.tile([P, P], F32, name="ident", align_bytes=64)
         make_identity(nc, ident[:])
-        neghalf = keep.tile([P, 4], F32, name="neghalf", align_bytes=64)
-        nc.gpsimd.memset(neghalf[:], -0.5)
+        zero_col = keep.tile([P, 1], F32, name="zero_col", align_bytes=64)
+        nc.gpsimd.memset(zero_col[:], 0.0)
         gb1_rows = keep.tile([P, P], BF16, name="gb1_rows", align_bytes=64)
         nc.gpsimd.memset(gb1_rows[:], 0.0)
         g0b = keep.tile([P, G, 4], BF16, name="g0b", align_bytes=64)
@@ -198,26 +198,32 @@ def tile_nodeupdatenetwork_pb_w8_kernel(
                 in_=w0s_raw[:, g * OG : (g + 1) * OG].rearrange("p (m t) -> p m t", t=4),
             )
 
-        def coefficients(var, factor, mean, sign, gamma, beta, n, tag):
-            ve = wt([P, n], F32, tag + "ve", 2)
-            a = wt([P, n], F32, tag + "a", 4)
-            m = wt([P, n], F32, tag + "m", 2)
+        def inv_std(var, factor, n, tag):
+            r = wt([P, n], F32, tag + "r", 3)
+            nc.scalar.activation(out=r[:], in_=var, func=ACT.Abs_reciprocal_sqrt, scale=factor, bias=eps_col[:])
+            return r
+
+        def coef_a(r, gpm, n, tag):
+            a = wt([P, n, 2], F32, tag + "a", 4)
+            for i in range(n):
+                nc.vector.tensor_scalar(
+                    out=a[:, i, :], in0=gpm[:, i, :], scalar1=r[:, i : i + 1], scalar2=None, op0=ALU.mult
+                )
+            return a
+
+        def coef_b(a, mean, beta, n, tag):
             b = wt([P, n], F32, tag + "b", 4)
-            nc.gpsimd.tensor_scalar(out=ve[:], in0=var, scalar1=factor, scalar2=EPS, op0=ALU.mult, op1=ALU.add)
-            nc.gpsimd.tensor_tensor(out=ve[:], in0=ve[:], in1=neghalf[:, 0:n], op=ALU.pow)
-            nc.gpsimd.tensor_tensor(out=a[:], in0=ve[:], in1=gamma, op=ALU.mult)
-            nc.gpsimd.tensor_tensor(out=m[:], in0=mean, in1=a[:], op=ALU.mult)
-            nc.gpsimd.tensor_tensor(out=b[:], in0=beta, in1=m[:], op=sign)
-            return a, b
+            for i in range(n):
+                nc.vector.scalar_tensor_tensor(
+                    out=b[:, i : i + 1], in0=mean[i], scalar=a[:, i, 1:2], in1=beta[:, i : i + 1], op0=ALU.mult, op1=ALU.add
+                )
+            return b
 
         def bn_tile(halves, mv, i):
             bs = wt([P, 2, 6], F32, "bs", 3)
             for h in range(2):
                 nc.vector.bn_stats(out=bs[:, h, :], in_=halves[h][:])
             nc.vector.bn_aggr(out=mv[:, i, :], in_=bs[:].rearrange("p h s -> p (h s)"))
-
-        def bn_coefficients(mv, gamma, beta, n, tag):
-            return coefficients(mv[:, :, 1], 1.0, mv[:, :, 0], ALU.subtract, gamma, beta, n, tag)
 
         y = {}
         v = {}
@@ -245,17 +251,11 @@ def tile_nodeupdatenetwork_pb_w8_kernel(
             if g not in v:
                 v[g] = wt([P, 4, R], F32, "v", 2)
 
-        def gb0(g, pair):
-            return g0f[:, g, 2 * pair : 2 * pair + 2], b0f[:, g, 2 * pair : 2 * pair + 2]
-
         def bn0(g, t):
             pair, i = t // 2, t % 2
             if i == 0:
                 part[g, pair] = wt([P, 2, 2], F32, "mv", 3)
             bn_tile(y[g, t], part[g, pair], i)
-            if i == 1:
-                gamma, beta = gb0(g, pair)
-                coef[g, pair] = bn_coefficients(part[g, pair], gamma, beta, 2, "c")
 
         def apply_psum(g, t, halves=(0, 1)):
             v_tile(g)
@@ -267,7 +267,7 @@ def tile_nodeupdatenetwork_pb_w8_kernel(
                     in_=y[g, t][h][:],
                     func=ACT.Identity,
                     bias=b[:, i : i + 1],
-                    scale=a[:, i : i + 1],
+                    scale=a[:, i, 0:1],
                 )
 
         def sum0(g, t):
@@ -283,31 +283,52 @@ def tile_nodeupdatenetwork_pb_w8_kernel(
                     func=ACT.Copy,
                     accum_out=sm[:, i, h : h + 1],
                 )
-            if i == 1:
-                tot = wt([P, 2], F32, "tot", 2)
-                nm = wt([P, 2], F32, "nm", 3)
-                nc.gpsimd.tensor_tensor(out=tot[:], in0=sm[:, :, 0], in1=sm[:, :, 1], op=ALU.add)
-                nc.gpsimd.tensor_scalar(
-                    out=nm[:], in0=tot[:], scalar1=-1.0 / R, scalar2=0.0, op0=ALU.mult, op1=ALU.add
-                )
-                part[g, pair] = (nm, wt([P, 2], F32, "sq", 3))
+
+        def total0(g, pair):
+            sm = part[g, pair]
+            tot = wt([P, 2], F32, "tot", 3)
+            nc.vector.tensor_tensor(out=tot[:], in0=sm[:, :, 0], in1=sm[:, :, 1], op=ALU.add)
+            part[g, pair] = (tot, wt([P, 2], F32, "sq", 3))
 
         def square0(g, t):
             pair, i = t // 2, t % 2
-            nm, sq = part[g, pair]
+            tot, sq = part[g, pair]
             junk = wt([P, R], BF16, "junk", 1)
             nc.scalar.activation(
-                out=junk[:], in_=v[g][:, t, :], func=ACT.Square, bias=nm[:, i : i + 1], accum_out=sq[:, i : i + 1]
+                out=junk[:],
+                in_=v[g][:, t, :],
+                func=ACT.Square,
+                scale=-float(R),
+                bias=tot[:, i : i + 1],
+                accum_out=sq[:, i : i + 1],
             )
-            if i == 1:
-                gamma, beta = gb0(g, pair)
-                coef[g, pair] = coefficients(sq[:], 1.0 / R, nm[:], ALU.add, gamma, beta, 2, "c")
+
+        def std0(g, pair):
+            if (g, pair) in VSTATS:
+                var, factor = part[g, pair][:, :, 1], 1.0
+            else:
+                var, factor = part[g, pair][1][:], 1.0 / R**3
+            coef[g, pair] = inv_std(var, factor, 2, "c")
+
+        def slope0(g, pair):
+            coef[g, pair] = coef_a(coef[g, pair], g0pm[:, g, 2 * pair : 2 * pair + 2, :], 2, "c")
+
+        def shift0(g, pair):
+            if (g, pair) in VSTATS:
+                mean = [part[g, pair][:, i, 0:1] for i in range(2)]
+            else:
+                tot = part[g, pair][0]
+                m = wt([P, 2], F32, "mean", 2)
+                nc.vector.tensor_scalar(out=m[:], in0=tot[:], scalar1=1.0 / R, scalar2=None, op0=ALU.mult)
+                mean = [m[:, i : i + 1] for i in range(2)]
+            a = coef[g, pair]
+            coef[g, pair] = (a, coef_b(a, mean, b0f[:, g, 2 * pair : 2 * pair + 2], 2, "c"))
 
         def apply_sbuf(g, t):
             a, b = coef[g, t // 2]
             i = t % 2
             nc.scalar.activation(
-                out=v[g][:, t, :], in_=v[g][:, t, :], func=ACT.Identity, bias=b[:, i : i + 1], scale=a[:, i : i + 1]
+                out=v[g][:, t, :], in_=v[g][:, t, :], func=ACT.Identity, bias=b[:, i : i + 1], scale=a[:, i, 0:1]
             )
 
         hg = {}
@@ -350,55 +371,82 @@ def tile_nodeupdatenetwork_pb_w8_kernel(
         w2 = {}
         coef2 = {}
 
-        def norm1(ct):
-            mv = wt([P, 1, 2], F32, "mv1", 3)
-            bn_tile(y2[ct], mv, 0)
-            coef2[ct] = bn_coefficients(mv, gb1[:, ct : ct + 1], gb1[:, 8 + ct : 9 + ct], 1, "d")
+        mv1 = {}
 
-        def apply1(ct):
-            v2[ct] = wt([P, R], F32, "xg", 2)
-            w2[ct] = wt([P, R], F32, "xq", 6)
+        def bn1(ct):
+            mv1[ct] = wt([P, 1, 2], F32, "mv1", 3)
+            bn_tile(y2[ct], mv1[ct], 0)
+
+        def std1(ct):
+            coef2[ct] = inv_std(mv1[ct][:, :, 1], 1.0, 1, "d")
+
+        def slope1(ct):
+            coef2[ct] = coef_a(coef2[ct], g1pm[:, ct : ct + 1, :], 1, "d")
+
+        def shift1(ct):
+            a = coef2[ct]
+            coef2[ct] = (a, coef_b(a, [mv1[ct][:, 0, 0:1]], gb1[:, 8 + ct : 9 + ct], 1, "d"))
+
+        def apply1(ct, h):
+            if h == 0:
+                v2[ct] = wt([P, R], F32, "xg", 2)
             a, b = coef2[ct]
-            for h in range(2):
-                cols = slice(HALF * h, HALF * (h + 1))
-                nc.scalar.activation(
-                    out=v2[ct][:, cols], in_=y2[ct][h][:], func=ACT.Identity, bias=b[:, 0:1], scale=a[:, 0:1]
-                )
-                nc.vector.scalar_tensor_tensor(
-                    out=w2[ct][:, cols], in0=v2[ct][:, cols], scalar=SLOPE, in1=v2[ct][:, cols], op0=ALU.mult, op1=ALU.max
-                )
+            cols = slice(HALF * h, HALF * (h + 1))
+            nc.scalar.activation(
+                out=v2[ct][:, cols], in_=y2[ct][h][:], func=ACT.Identity, bias=b[:, 0:1], scale=a[:, 0, 0:1]
+            )
+
+        def leaky1(ct, h):
+            if h == 0:
+                w2[ct] = wt([P, R], F32, "xq", 6)
+            cols = slice(HALF * h, HALF * (h + 1))
+            nc.vector.scalar_tensor_tensor(
+                out=w2[ct][:, cols], in0=v2[ct][:, cols], scalar=SLOPE, in1=v2[ct][:, cols], op0=ALU.mult, op1=ALU.max
+            )
 
         o = {}
 
-        def store(ct):
-            if ct % 2 == 0:
+        ots = {}
+
+        def turn1(ct, h):
+            ot = psum.tile([P, 4, P], F32, name="acc", tag="acc", bufs=4)
+            for q in range(4):
+                b = 4 * h + q
+                nc.tensor.transpose(ot[:, q, :], w2[ct][:, P * b : P * (b + 1)], ident[:])
+            ots[ct, h] = ot
+
+        def store(ct, h):
+            if ct % 2 == 0 and h == 0:
                 o[ct // 2] = wt([P, NB, 2 * P], F32, "xb", 6)
             ob = o[ct // 2]
             lo = P * (ct % 2)
-            for h in range(2):
-                ot = psum.tile([P, 4, P], F32, name="acc", tag="acc", bufs=4)
-                for q in range(4):
-                    b = 4 * h + q
-                    nc.tensor.transpose(ot[:, q, :], w2[ct][:, P * b : P * (b + 1)], ident[:])
-                nc.scalar.copy(out=ob[:, 4 * h : 4 * h + 4, lo : lo + P], in_=ot[:])
-                if ct % 2 == 1:
-                    nc.sync.dma_start(
-                        out=out_v[:, 4 * h : 4 * h + 4, P * (ct - 1) : P * (ct + 1)], in_=ob[:, 4 * h : 4 * h + 4, :]
-                    )
+            nc.scalar.copy(out=ob[:, 4 * h : 4 * h + 4, lo : lo + P], in_=ots[ct, h][:])
+            if ct % 2 == 1:
+                nc.sync.dma_start(
+                    out=out_v[:, 4 * h : 4 * h + 4, P * (ct - 1) : P * (ct + 1)], in_=ob[:, 4 * h : 4 * h + 4, :]
+                )
 
-        g0f = keep.tile([P, G, 4], F32, name="g0f", align_bytes=64)
+        g0pm = keep.tile([P, G, 4, 2], F32, name="g0pm", align_bytes=64)
         b0f = keep.tile([P, G, 4], F32, name="b0f", align_bytes=64)
-        nc.gpsimd.tensor_copy(out=g0f[:], in_=g0b[:])
+        nc.gpsimd.tensor_copy(out=g0pm[:, :, :, 0], in_=g0b[:])
+        nc.gpsimd.tensor_scalar(out=g0pm[:, :, :, 1], in0=g0b[:], scalar1=-1.0, scalar2=0.0, op0=ALU.mult, op1=ALU.add)
         nc.gpsimd.tensor_copy(out=b0f[:], in_=b0b[:])
+        eps_col = keep.tile([P, 1], F32, name="eps_col", align_bytes=64)
+        nc.gpsimd.tensor_scalar(out=eps_col[:], in0=zero_col[:], scalar1=1.0, scalar2=EPS, op0=ALU.mult, op1=ALU.add)
         gb1_f = keep.tile([P, P], F32, name="gb1_f", align_bytes=64)
         nc.gpsimd.tensor_copy(out=gb1_f[:], in_=gb1_rows[:])
         gb1 = keep.tile([P, 16], F32, name="gb1", align_bytes=64)
+        g1pm = keep.tile([P, 8, 2], F32, name="g1pm", align_bytes=64)
         w1 = keep.tile([P, 4, C1], I32, name="w1", align_bytes=64)
 
         steps = {}
+        early = {}
 
         def at(step, fn, *args):
             steps.setdefault(step, []).append((fn, args))
+
+        def before(step, fn, *args):
+            early.setdefault(step, []).append((fn, args))
 
         for c in range(12):
             if c < 11:
@@ -413,15 +461,23 @@ def tile_nodeupdatenetwork_pb_w8_kernel(
                 at(s - 1, conv0, g, 0)
                 at(s, conv0, g, 1)
                 if on_vector == (True, True):
-                    plan = [(0, bn0, 0), (1, bn0, 1), (3, apply_psum, 0), (4, apply_psum, 1), (4, conv0, 2), (5, conv0, 3)]
-                    plan += [(5, bn0, 2), (6, bn0, 3), (8, apply_psum, 2), (9, apply_psum, 3)]
+                    plan = [(0, bn0, 0), (1, bn0, 1), (2, std0, 0), (2, slope0, 0), (3, apply_psum, 0), (4, apply_psum, 1)]
+                    plan += [(4, conv0, 2), (5, conv0, 3), (5, bn0, 2), (6, bn0, 3), (7, std0, 1), (7, slope0, 1)]
+                    plan += [(8, apply_psum, 2), (9, apply_psum, 3)]
+                    first = [(3, shift0, 0), (8, shift0, 1)]
                 elif on_vector == (False, True):
                     plan = [(0, sum0, 0), (1, sum0, 1), (1, conv0, 2), (2, conv0, 3), (2, bn0, 2), (3, bn0, 3)]
-                    plan += [(2, square0, 0), (3, square0, 1)]
-                    plan += [(5, apply_psum, 2), (6, apply_psum, 3), (7, apply_sbuf, 0), (8, apply_sbuf, 1)]
+                    plan += [(3, square0, 0), (4, square0, 1), (4, std0, 1), (4, slope0, 1), (5, std0, 0), (5, slope0, 0)]
+                    plan += [(6, apply_psum, 2), (7, apply_psum, 3), (8, apply_sbuf, 0), (9, apply_sbuf, 1)]
+                    first = [(2, total0, 0), (5, shift0, 1), (6, shift0, 0)]
                 else:
                     plan = [(0, sum0, 0), (1, sum0, 1), (1, conv0, 2), (2, conv0, 3), (2, sum0, 2), (3, sum0, 3)]
-                    plan += [(4 + t, square0, t) for t in range(4)] + [(8 + t, apply_sbuf, t) for t in range(4)]
+                    plan += [(4, square0, 0), (5, square0, 1), (6, std0, 0), (6, square0, 2), (6, slope0, 0), (7, square0, 3)]
+                    plan += [(8, std0, 1), (8, apply_sbuf, 0), (8, slope0, 1)]
+                    plan += [(9, apply_sbuf, 1), (10, apply_sbuf, 2), (11, apply_sbuf, 3)]
+                    first = [(2, total0, 0), (4, total0, 1), (7, shift0, 0), (9, shift0, 1)]
+                for k, fn, t in first:
+                    before(s + k, fn, g, t)
                 for k, fn, t in plan:
                     at(s + k, fn, g, t)
                 s += plan[-1][0]
@@ -444,6 +500,8 @@ def tile_nodeupdatenetwork_pb_w8_kernel(
             gpt = psum.tile([P, P], F32, name="pt", tag="pt", bufs=4)
             nc.tensor.transpose(gpt[:], gb1_f[:], ident[:])
             nc.scalar.copy(out=gb1[:], in_=gpt[:, 0:16])
+            nc.scalar.copy(out=g1pm[:, :, 0], in_=gpt[:, 0:8])
+            nc.scalar.mul(out=g1pm[:, :, 1], in_=gpt[:, 0:8], mul=-1.0)
 
         at(G3, load_group3)
         at(20, load_w1)
@@ -463,6 +521,8 @@ def tile_nodeupdatenetwork_pb_w8_kernel(
             if s + 2 < 48:
                 turn(s + 2)
             empty(s)
+            for fn, args in early.get(s, []):
+                fn(*args)
             k = (s + 1) / 12
             lo = int(k)
             fill(int(RATE[lo] + (k - lo) * (RATE[min(4, lo + 1)] - RATE[lo])))
@@ -472,25 +532,39 @@ def tile_nodeupdatenetwork_pb_w8_kernel(
         quant(11)
         for t in range(4):
             conv0(3, t, "acc" if t < 2 else "pt")
-        for t in range(4):
-            bn0(3, t)
-        for s in range(48, 80):
-            for fn, args in steps.get(s, []):
-                if fn in (square0, apply_psum, apply_sbuf):
-                    fn(*args)
-        for s in range(48, 80):
-            for fn, args in steps.get(s, []):
-                if fn in (leaky0, quant_h):
-                    fn(*args)
+        rest = [(fn, args) for s in range(48, 90) for fn, args in early.get(s, []) + steps.get(s, [])]
+        late = [x for x in rest if x[0] in (leaky0, quant_h)]
+        for fn, args in rest:
+            if fn not in (leaky0, quant_h):
+                fn(*args)
+        bn0(3, 0)
+        bn0(3, 1)
+        std0(3, 0)
+        bn0(3, 2)
+        slope0(3, 0)
+        bn0(3, 3)
+        shift0(3, 0)
+        std0(3, 1)
         for h in range(2):
             for t in range(2):
                 apply_psum(3, t, (h,))
         for ct in range(2):
             for h in range(2):
-                conv1(ct, h, range(0, 3))
+                conv1(ct, h, range(0, 2))
+        for fn, args in late[:1]:
+            fn(*args)
+        slope0(3, 1)
+        for fn, args in late[1:2]:
+            fn(*args)
+        shift0(3, 1)
+        for fn, args in late[2:]:
+            fn(*args)
         for h in range(2):
             for t in range(2, 4):
                 apply_psum(3, t, (h,))
+        for ct in range(2):
+            for h in range(2):
+                conv1(ct, h, range(2, 3))
         for ct in range(2, 4):
             for h in range(2):
                 conv1(ct, h, range(0, 3))
@@ -499,12 +573,28 @@ def tile_nodeupdatenetwork_pb_w8_kernel(
         quant_h(3, 0)
         quant_h(3, 1)
 
-        for s in range(11):
-            if 0 <= s - 2 < 8:
-                apply1(s - 2)
-            if s < 8:
+        for s in range(12):
+            a, b, c, d = s, s - 1, s - 2, s - 3
+            if 0 <= b < 8:
+                std1(b)
+            if 0 <= c < 8:
+                leaky1(c, 0)
+            if 0 <= b < 8:
+                slope1(b)
+            if 0 <= c < 8:
+                leaky1(c, 1)
+            if 0 <= b < 8:
+                shift1(b)
+            if 0 <= d < 8:
+                store(d, 0)
+                store(d, 1)
+            if 0 <= b < 8:
+                apply1(b, 0)
+                apply1(b, 1)
+            if a < 8:
                 for h in range(2):
-                    conv1(s, h, range(3, 4) if s < 4 else range(0, 4))
-                norm1(s)
-            if 0 <= s - 3 < 8:
-                store(s - 3)
+                    conv1(a, h, range(3, 4) if a < 4 else range(0, 4))
+                bn1(a)
+            if 0 <= c < 8:
+                turn1(c, 0)
+                turn1(c, 1)

from contextlib import ExitStack

import concourse.mybir as mybir
from concourse.masks import make_identity

R, C0, C1 = 1024, 2048, 1024
F, EF = 2048, 4096
G, CG, OG = 4, 1536, 512
EPS = 1e-5
SLOPE = 0.01
FLOPS = 2 * R * CG * C0 + 2 * R * C0 * C1

P = 128
KC = 512
NB = R // P
HALF = 512

F32 = mybir.dt.float32
BF16 = mybir.dt.bfloat16
U32 = mybir.dt.uint32
I32 = mybir.dt.int32
U8 = mybir.dt.uint8
FP8 = mybir.dt.float8_e4m3fn
FP8X4 = mybir.dt.float8_e4m3fn_x4
ALU = mybir.AluOpType
ACT = mybir.ActivationFunctionType

VSTATS = {(0, 1), (1, 1), (3, 0), (3, 1)}
CONV = [2, 2, 2]
SOP = [6,4,6]
LOFF = [12,3,10]
QOFF = 2
HEAD = ["n2","n0a","w","n0b","a1a","n1","a1b","ws","a2a","n3","a2b"]
PERM = [7,4,3,5]
SPREAD = [4,5,3,12,15,19]
G3 = 11
RATE = [8,20,44,64,64]


def tile_nodeupdatenetwork_pb_w8_kernel(
    tc, node_feat, aggr_bytes, aggr_scale, w0_words, w0_scales, gamma0, beta0, w1_words, w1_scales, gamma1, beta1, out
):
    nc = tc.nc
    node_v = node_feat.flatten_outer_dims().rearrange("(b p) k -> p b k", p=P)
    aggr_v = aggr_bytes.flatten_outer_dims().rearrange("(b p) k -> p b k", p=P)
    scale_v = aggr_scale.rearrange("a b k -> (a b k)")
    w0_v = w0_words.bitcast(I32).rearrange("g p n o -> p g (n o)")
    w1_v = w1_words.bitcast(I32).rearrange("g p n o -> p g (n o)")
    out_v = out.flatten_outer_dims().rearrange("(b p) c -> p b c", p=P)

    with ExitStack() as ctx:
        keep = ctx.enter_context(tc.tile_pool(name="keep", bufs=1))
        work = ctx.enter_context(tc.tile_pool(name="work", bufs=2))
        psum = ctx.enter_context(tc.psum_pool(name="psum", bufs=4))

        def wt(shape, dtype, tag, bufs):
            return work.tile(shape, dtype, name=tag, tag=tag, bufs=bufs, align_bytes=64)

        ctx.enter_context(tc.manual_schedule())
        w0s_raw = keep.tile([P, C0], U8, name="w0s_raw", align_bytes=64)
        w1s = keep.tile([P, C1], U8, name="w1s", align_bytes=64)
        nc.vector.memset(w0s_raw[:].bitcast(I32), 0)
        nc.vector.memset(w1s[:].bitcast(I32), 0)
        ident = keep.tile([P, P], F32, name="ident", align_bytes=64)
        make_identity(nc, ident[:])
        zero_col = keep.tile([P, 1], F32, name="zero_col", align_bytes=64)
        nc.gpsimd.memset(zero_col[:], 0.0)
        gb1_rows = keep.tile([P, P], BF16, name="gb1_rows", align_bytes=64)
        nc.gpsimd.memset(gb1_rows[:], 0.0)
        g0b = keep.tile([P, G, 4], BF16, name="g0b", align_bytes=64)
        b0b = keep.tile([P, G, 4], BF16, name="b0b", align_bytes=64)
        nc.scalar.dma_start(out=g0b[:], in_=gamma0.rearrange("(g p t) -> p g t", p=P, t=4))
        nc.scalar.dma_start(out=b0b[:], in_=beta0.rearrange("(g p t) -> p g t", p=P, t=4))
        nc.scalar.dma_start(out=gb1_rows[0:8, :], in_=gamma1.rearrange("(c p) -> c p", p=P))
        nc.scalar.dma_start(out=gb1_rows[8:16, :], in_=beta1.rearrange("(c p) -> c p", p=P))

        xb = {}
        ab = {}
        sc = {}
        w0raw = {}

        def chunk_tile(c):
            xb[c] = wt([P, NB, KC], BF16, "xb", 6)

        def load_node(c, b0, b1):
            nc.sync.dma_start(out=xb[c][:, b0:b1, :], in_=node_v[:, b0:b1, c * KC : (c + 1) * KC])

        def aggr_cols(g):
            lo = max(0, g * CG - F)
            return lo, (g + 1) * CG - F

        def aggr_tiles(g):
            lo, hi = aggr_cols(g)
            ab[g] = wt([P, NB, hi - lo], U8, "ab", 2)
            sc[g] = wt([P, hi - lo], F32, "sc", 2)

        def load_aggr(g, b0, b1):
            lo, hi = aggr_cols(g)
            nc.sync.dma_start(out=ab[g][:, b0:b1, :], in_=aggr_v[:, b0:b1, lo:hi])

        scale_rows = keep.tile([P, P], F32, name="scale_rows", align_bytes=64)
        nc.vector.memset(scale_rows[:], 0.0)
        nc.sync.dma_start(out=scale_rows[0 : EF // P, :], in_=scale_v.rearrange("(m n) -> m n", n=P))
        scale_cols = keep.tile([P, EF // P], F32, name="scale_cols", align_bytes=64)

        def spread_scale(c):
            g = c // 3
            lo = c * KC - F
            pt = psum.tile([P, 4, P], F32, name="pt", tag="pt", bufs=4)
            for q in range(4):
                m = lo // P + q
                nc.tensor.transpose(pt[:, q, :], scale_cols[:, m : m + 1].to_broadcast([P, P]), ident[:])
            rel = lo - aggr_cols(g)[0]
            nc.scalar.copy(out=sc[g][:, rel : rel + KC], in_=pt[:].rearrange("p q n -> p (q n)"))


        def load_w0(g):
            w0raw[g] = wt([P, 3, OG], I32, "w0raw", 1)
            nc.sync.dma_start(out=w0raw[g][:], in_=w0_v[:, :, g * OG : (g + 1) * OG])

        def load_plane(tile, scales, passes):
            sv = scales.bitcast(I32)
            for q in range(4):
                nc.sync.dma_start(out=tile[32 * q : 32 * q + 4 * passes, :].bitcast(I32), in_=sv[:, 4 * q : 4 * q + 4, :])

        aggr_tiles(1)
        for c in range(4):
            chunk_tile(c)
        aggr_tiles(2)
        loads = {
            "a1a": (load_aggr, 1, 0, 4), "a1b": (load_aggr, 1, 4, 8),
            "n0a": (load_node, 0, 0, 4), "n0b": (load_node, 0, 4, 8), "n1": (load_node, 1, 0, 8), "n2": (load_node, 2, 0, 8), "n3": (load_node, 3, 0, 8),
            "a2a": (load_aggr, 2, 0, 4), "a2b": (load_aggr, 2, 4, 8), "w": (load_w0, 0), "ws": (load_plane, w0s_raw, w0_scales, 3),
        }
        for name in HEAD:
            fn, *args = loads[name]
            fn(*args)

        pieces = [(c, b) for c in range(4, 12) for b in range(NB)]
        pos = [0]

        def fill(upto):
            for c, b in pieces[pos[0] : upto]:
                if b == 0:
                    chunk_tile(c)
                g = c // 3
                lo = c * KC - F - aggr_cols(g)[0]
                nc.vector.tensor_tensor(
                    out=xb[c][:, b, :],
                    in0=ab[g][:, b, lo : lo + KC].bitcast(FP8),
                    in1=sc[g][:, lo : lo + KC],
                    op=ALU.mult,
                )
            pos[0] = max(pos[0], min(upto, len(pieces)))

        xg = {}

        pts = {}

        def turn(s):
            c, bank = s // 4, s % 4
            words = xb[c][:].rearrange("p b k -> p (b k)").bitcast(F32)
            pt = psum.tile([P, 2, 2, P], F32, name="pt", tag="pt", bufs=4)
            for q in range(2):
                b = 2 * bank + q
                for u in range(2):
                    nc.tensor.transpose(pt[:, q, u, :], words[:, 256 * b + u : 256 * (b + 1) : 2], ident[:])
            pts[s] = pt

        def empty(s):
            c, bank = s // 4, s % 4
            if bank == 0:
                xg[c] = wt([P, R * 4], BF16, "xg", 2)
            dst = xg[c][:].bitcast(F32).rearrange("p (b r u) -> p b r u", r=P, u=2)
            nc.scalar.copy(out=dst[:, 2 * bank : 2 * bank + 2], in_=pts[s][:].rearrange("p q u r -> p q r u"))

        xq = {}
        xs = {}

        def quant(c):
            xq[c] = wt([P, R], U32, "xq", 6)
            xs[c] = wt([P, R], U8, "xs", 6)
            nc.vector.quantize_mx(out=xq[c][:].bitcast(FP8X4), scales=xs[c][:], in_=xg[c][:])

        w0p = {}
        w0s = {}

        def permute(g):
            w0p[g] = wt([P, 3, OG], I32, "w0p", 2)
            w0s[g] = wt([P, OG], U8, "w0s", 2)
            for j in range(3):
                nc.vector.tensor_copy(
                    out=w0p[g][:, j, :].rearrange("p (t m) -> p m t", t=4),
                    in_=w0raw[g][:, j, :].rearrange("p (m t) -> p m t", t=4),
                )
            nc.vector.tensor_copy(
                out=w0s[g][:].rearrange("p (t m) -> p m t", t=4),
                in_=w0s_raw[:, g * OG : (g + 1) * OG].rearrange("p (m t) -> p m t", t=4),
            )

        def inv_std(var, factor, n, tag):
            r = wt([P, n], F32, tag + "r", 3)
            nc.scalar.activation(out=r[:], in_=var, func=ACT.Abs_reciprocal_sqrt, scale=factor, bias=eps_col[:])
            return r

        def coef_a(r, gpm, n, tag):
            a = wt([P, n, 2], F32, tag + "a", 4)
            for i in range(n):
                nc.vector.tensor_scalar(
                    out=a[:, i, :], in0=gpm[:, i, :], scalar1=r[:, i : i + 1], scalar2=None, op0=ALU.mult
                )
            return a

        def coef_b(a, mean, beta, n, tag):
            b = wt([P, n], F32, tag + "b", 4)
            for i in range(n):
                nc.vector.scalar_tensor_tensor(
                    out=b[:, i : i + 1], in0=mean[i], scalar=a[:, i, 1:2], in1=beta[:, i : i + 1], op0=ALU.mult, op1=ALU.add
                )
            return b

        def bn_tile(halves, mv, i):
            bs = wt([P, 2, 6], F32, "bs", 3)
            for h in range(2):
                nc.vector.bn_stats(out=bs[:, h, :], in_=halves[h][:])
            nc.vector.bn_aggr(out=mv[:, i, :], in_=bs[:].rearrange("p h s -> p (h s)"))

        y = {}
        v = {}
        coef = {}
        part = {}

        def conv0(g, t, tag="acc"):
            y[g, t] = []
            for h in range(2):
                acc = psum.tile([P, HALF], F32, name=tag, tag=tag, bufs=4)
                for j in range(3):
                    c = 3 * g + j
                    nc.tensor.matmul_mx(
                        out=acc[:],
                        lhsT=w0p[g][:, j, P * t : P * (t + 1)].bitcast(FP8X4),
                        lhsT_scale=w0s[g][4 * j : P, P * t : P * (t + 1)],
                        rhs=xq[c][:, HALF * h : HALF * (h + 1)].bitcast(FP8X4),
                        rhs_scale=xs[c][:, HALF * h : HALF * (h + 1)],
                        start=(j == 0),
                        stop=(j == 2),
                    )
                y[g, t].append(acc)

        def v_tile(g):
            if g not in v:
                v[g] = wt([P, 4, R], F32, "v", 2)

        def bn0(g, t):
            pair, i = t // 2, t % 2
            if i == 0:
                part[g, pair] = wt([P, 2, 2], F32, "mv", 3)
            bn_tile(y[g, t], part[g, pair], i)

        def apply_psum(g, t, halves=(0, 1)):
            v_tile(g)
            a, b = coef[g, t // 2]
            i = t % 2
            for h in halves:
                nc.scalar.activation(
                    out=v[g][:, t, HALF * h : HALF * (h + 1)],
                    in_=y[g, t][h][:],
                    func=ACT.Identity,
                    bias=b[:, i : i + 1],
                    scale=a[:, i, 0:1],
                )

        def sum0(g, t):
            v_tile(g)
            pair, i = t // 2, t % 2
            if i == 0:
                part[g, pair] = wt([P, 2, 2], F32, "sm", 3)
            sm = part[g, pair]
            for h in range(2):
                nc.scalar.activation(
                    out=v[g][:, t, HALF * h : HALF * (h + 1)],
                    in_=y[g, t][h][:],
                    func=ACT.Copy,
                    accum_out=sm[:, i, h : h + 1],
                )

        def total0(g, pair):
            sm = part[g, pair]
            tot = wt([P, 2], F32, "tot", 3)
            nc.vector.tensor_tensor(out=tot[:], in0=sm[:, :, 0], in1=sm[:, :, 1], op=ALU.add)
            part[g, pair] = (tot, wt([P, 2], F32, "sq", 3))

        def square0(g, t):
            pair, i = t // 2, t % 2
            tot, sq = part[g, pair]
            junk = wt([P, R], BF16, "junk", 1)
            nc.scalar.activation(
                out=junk[:],
                in_=v[g][:, t, :],
                func=ACT.Square,
                scale=-float(R),
                bias=tot[:, i : i + 1],
                accum_out=sq[:, i : i + 1],
            )

        def std0(g, pair):
            if (g, pair) in VSTATS:
                var, factor = part[g, pair][:, :, 1], 1.0
            else:
                var, factor = part[g, pair][1][:], 1.0 / R**3
            coef[g, pair] = inv_std(var, factor, 2, "c")

        def slope0(g, pair):
            coef[g, pair] = coef_a(coef[g, pair], g0pm[:, g, 2 * pair : 2 * pair + 2, :], 2, "c")

        def shift0(g, pair):
            if (g, pair) in VSTATS:
                mean = [part[g, pair][:, i, 0:1] for i in range(2)]
            else:
                tot = part[g, pair][0]
                m = wt([P, 2], F32, "mean", 2)
                nc.vector.tensor_scalar(out=m[:], in0=tot[:], scalar1=1.0 / R, scalar2=None, op0=ALU.mult)
                mean = [m[:, i : i + 1] for i in range(2)]
            a = coef[g, pair]
            coef[g, pair] = (a, coef_b(a, mean, b0f[:, g, 2 * pair : 2 * pair + 2], 2, "c"))

        def apply_sbuf(g, t):
            a, b = coef[g, t // 2]
            i = t % 2
            nc.scalar.activation(
                out=v[g][:, t, :], in_=v[g][:, t, :], func=ACT.Identity, bias=b[:, i : i + 1], scale=a[:, i, 0:1]
            )

        hg = {}
        hq = {}
        hs = {}

        def leaky0(g, h):
            hg[g, h] = wt([P, HALF, 4], BF16, "hg", 2)
            vin = v[g][:, :, HALF * h : HALF * (h + 1)].rearrange("p t r -> p r t")
            nc.vector.scalar_tensor_tensor(out=hg[g, h][:], in0=vin, scalar=SLOPE, in1=vin, op0=ALU.mult, op1=ALU.max)

        def quant_h(g, h):
            if h == 0:
                hq[g] = keep.tile([P, R], U32, name="hq%d" % g, align_bytes=64)
                hs[g] = keep.tile([P, R], U8, name="hs%d" % g, align_bytes=64)
            nc.vector.quantize_mx(
                out=hq[g][:, HALF * h : HALF * (h + 1)].bitcast(FP8X4),
                scales=hs[g][:, HALF * h : HALF * (h + 1)],
                in_=hg[g, h][:].rearrange("p r t -> p (r t)"),
            )

        y2 = {}

        def conv1(ct, h, passes):
            if ct not in y2:
                tag = "acc" if ct in (0, 1, 4, 7) else "pt"
                y2[ct] = [psum.tile([P, HALF], F32, name=tag, tag=tag, bufs=4) for i in range(2)]
            for g in passes:
                nc.tensor.matmul_mx(
                    out=y2[ct][h][:],
                    lhsT=w1[:, g, P * ct : P * (ct + 1)].bitcast(FP8X4),
                    lhsT_scale=w1s[4 * g : P, P * ct : P * (ct + 1)],
                    rhs=hq[g][:, HALF * h : HALF * (h + 1)].bitcast(FP8X4),
                    rhs_scale=hs[g][:, HALF * h : HALF * (h + 1)],
                    start=(g == 0),
                    stop=(g == 3),
                )

        v2 = {}
        w2 = {}
        coef2 = {}

        mv1 = {}

        def bn1(ct):
            mv1[ct] = wt([P, 1, 2], F32, "mv1", 3)
            bn_tile(y2[ct], mv1[ct], 0)

        def std1(ct):
            coef2[ct] = inv_std(mv1[ct][:, :, 1], 1.0, 1, "d")

        def slope1(ct):
            coef2[ct] = coef_a(coef2[ct], g1pm[:, ct : ct + 1, :], 1, "d")

        def shift1(ct):
            a = coef2[ct]
            coef2[ct] = (a, coef_b(a, [mv1[ct][:, 0, 0:1]], gb1[:, 8 + ct : 9 + ct], 1, "d"))

        def apply1(ct, h):
            if h == 0:
                v2[ct] = wt([P, R], F32, "xg", 2)
            a, b = coef2[ct]
            cols = slice(HALF * h, HALF * (h + 1))
            nc.scalar.activation(
                out=v2[ct][:, cols], in_=y2[ct][h][:], func=ACT.Identity, bias=b[:, 0:1], scale=a[:, 0, 0:1]
            )

        def leaky1(ct, h):
            if h == 0:
                w2[ct] = wt([P, R], F32, "xq", 6)
            cols = slice(HALF * h, HALF * (h + 1))
            nc.vector.scalar_tensor_tensor(
                out=w2[ct][:, cols], in0=v2[ct][:, cols], scalar=SLOPE, in1=v2[ct][:, cols], op0=ALU.mult, op1=ALU.max
            )

        o = {}

        ots = {}

        def turn1(ct, h):
            ot = psum.tile([P, 4, P], F32, name="acc", tag="acc", bufs=4)
            for q in range(4):
                b = 4 * h + q
                nc.tensor.transpose(ot[:, q, :], w2[ct][:, P * b : P * (b + 1)], ident[:])
            ots[ct, h] = ot

        def store(ct, h):
            if ct % 2 == 0 and h == 0:
                o[ct // 2] = wt([P, NB, 2 * P], F32, "xb", 6)
            ob = o[ct // 2]
            lo = P * (ct % 2)
            nc.scalar.copy(out=ob[:, 4 * h : 4 * h + 4, lo : lo + P], in_=ots[ct, h][:])
            if ct % 2 == 1:
                nc.sync.dma_start(
                    out=out_v[:, 4 * h : 4 * h + 4, P * (ct - 1) : P * (ct + 1)], in_=ob[:, 4 * h : 4 * h + 4, :]
                )

        g0pm = keep.tile([P, G, 4, 2], F32, name="g0pm", align_bytes=64)
        b0f = keep.tile([P, G, 4], F32, name="b0f", align_bytes=64)
        nc.gpsimd.tensor_copy(out=g0pm[:, :, :, 0], in_=g0b[:])
        nc.gpsimd.tensor_scalar(out=g0pm[:, :, :, 1], in0=g0b[:], scalar1=-1.0, scalar2=0.0, op0=ALU.mult, op1=ALU.add)
        nc.gpsimd.tensor_copy(out=b0f[:], in_=b0b[:])
        eps_col = keep.tile([P, 1], F32, name="eps_col", align_bytes=64)
        nc.gpsimd.tensor_scalar(out=eps_col[:], in0=zero_col[:], scalar1=1.0, scalar2=EPS, op0=ALU.mult, op1=ALU.add)
        gb1_f = keep.tile([P, P], F32, name="gb1_f", align_bytes=64)
        nc.gpsimd.tensor_copy(out=gb1_f[:], in_=gb1_rows[:])
        gb1 = keep.tile([P, 16], F32, name="gb1", align_bytes=64)
        g1pm = keep.tile([P, 8, 2], F32, name="g1pm", align_bytes=64)
        w1 = keep.tile([P, 4, C1], I32, name="w1", align_bytes=64)

        steps = {}
        early = {}

        def at(step, fn, *args):
            steps.setdefault(step, []).append((fn, args))

        def before(step, fn, *args):
            early.setdefault(step, []).append((fn, args))

        for c in range(12):
            if c < 11:
                at(4 * c + 3 + QOFF, quant, c)
        for g in range(G):
            base = 12 * (g + 1)
            at(base - PERM[g], permute, g)
            if g < 3:
                at(base - 1, load_w0, g + 1)
                on_vector = tuple((g, p) in VSTATS for p in range(2))
                s = base + SOP[g]
                at(s - 1, conv0, g, 0)
                at(s, conv0, g, 1)
                if on_vector == (True, True):
                    plan = [(0, bn0, 0), (1, bn0, 1), (2, std0, 0), (2, slope0, 0), (3, apply_psum, 0), (4, apply_psum, 1)]
                    plan += [(4, conv0, 2), (5, conv0, 3), (5, bn0, 2), (6, bn0, 3), (7, std0, 1), (7, slope0, 1)]
                    plan += [(8, apply_psum, 2), (9, apply_psum, 3)]
                    first = [(3, shift0, 0), (8, shift0, 1)]
                elif on_vector == (False, True):
                    plan = [(0, sum0, 0), (1, sum0, 1), (1, conv0, 2), (2, conv0, 3), (2, bn0, 2), (3, bn0, 3)]
                    plan += [(3, square0, 0), (4, square0, 1), (4, std0, 1), (4, slope0, 1), (5, std0, 0), (5, slope0, 0)]
                    plan += [(6, apply_psum, 2), (7, apply_psum, 3), (8, apply_sbuf, 0), (9, apply_sbuf, 1)]
                    first = [(2, total0, 0), (5, shift0, 1), (6, shift0, 0)]
                else:
                    plan = [(0, sum0, 0), (1, sum0, 1), (1, conv0, 2), (2, conv0, 3), (2, sum0, 2), (3, sum0, 3)]
                    plan += [(4, square0, 0), (5, square0, 1), (6, std0, 0), (6, square0, 2), (6, slope0, 0), (7, square0, 3)]
                    plan += [(8, std0, 1), (8, apply_sbuf, 0), (8, slope0, 1)]
                    plan += [(9, apply_sbuf, 1), (10, apply_sbuf, 2), (11, apply_sbuf, 3)]
                    first = [(2, total0, 0), (4, total0, 1), (7, shift0, 0), (9, shift0, 1)]
                for k, fn, t in first:
                    before(s + k, fn, g, t)
                for k, fn, t in plan:
                    at(s + k, fn, g, t)
                s += plan[-1][0]
                s += LOFF[g]
                at(s, leaky0, g, 0)
                at(s + 1, leaky0, g, 1)
                at(s + 1, quant_h, g, 0)
                at(s + 2, quant_h, g, 1)

        def load_group3():
            aggr_tiles(3)
            load_aggr(3, 0, 8)

        def load_w1():
            for half in range(2):
                nc.sync.dma_start(out=w1[:, 2 * half : 2 * half + 2, :], in_=w1_v[:, 2 * half : 2 * half + 2, :])
            load_plane(w1s, w1_scales, 4)

        def turn_gb1():
            gpt = psum.tile([P, P], F32, name="pt", tag="pt", bufs=4)
            nc.tensor.transpose(gpt[:], gb1_f[:], ident[:])
            nc.scalar.copy(out=gb1[:], in_=gpt[:, 0:16])
            nc.scalar.copy(out=g1pm[:, :, 0], in_=gpt[:, 0:8])
            nc.scalar.mul(out=g1pm[:, :, 1], in_=gpt[:, 0:8], mul=-1.0)

        at(G3, load_group3)
        at(20, load_w1)
        at(8, turn_gb1)

        spt = psum.tile([P, P], F32, name="pt", tag="pt", bufs=4)
        nc.tensor.transpose(spt[:], scale_rows[:], ident[:])
        nc.scalar.copy(out=scale_cols[:], in_=spt[:, 0 : EF // P])
        spread_scale(4)
        spread_scale(5)
        for c in range(6, 12):
            at(SPREAD[c - 6], spread_scale, c)
        fill(8)
        turn(0)
        turn(1)
        for s in range(48):
            if s + 2 < 48:
                turn(s + 2)
            empty(s)
            for fn, args in early.get(s, []):
                fn(*args)
            k = (s + 1) / 12
            lo = int(k)
            fill(int(RATE[lo] + (k - lo) * (RATE[min(4, lo + 1)] - RATE[lo])))
            for fn, args in steps.get(s, []):
                fn(*args)

        quant(11)
        for t in range(4):
            conv0(3, t, "acc" if t < 2 else "pt")
        rest = [(fn, args) for s in range(48, 90) for fn, args in early.get(s, []) + steps.get(s, [])]
        late = [x for x in rest if x[0] in (leaky0, quant_h)]
        for fn, args in rest:
            if fn not in (leaky0, quant_h):
                fn(*args)
        bn0(3, 0)
        bn0(3, 1)
        std0(3, 0)
        bn0(3, 2)
        slope0(3, 0)
        bn0(3, 3)
        shift0(3, 0)
        std0(3, 1)
        for h in range(2):
            for t in range(2):
                apply_psum(3, t, (h,))
        for ct in range(2):
            for h in range(2):
                conv1(ct, h, range(0, 2))
        for fn, args in late[:1]:
            fn(*args)
        slope0(3, 1)
        for fn, args in late[1:2]:
            fn(*args)
        shift0(3, 1)
        for fn, args in late[2:]:
            fn(*args)
        for h in range(2):
            for t in range(2, 4):
                apply_psum(3, t, (h,))
        for ct in range(2):
            for h in range(2):
                conv1(ct, h, range(2, 3))
        for ct in range(2, 4):
            for h in range(2):
                conv1(ct, h, range(0, 3))
        leaky0(3, 0)
        leaky0(3, 1)
        quant_h(3, 0)
        quant_h(3, 1)

        for s in range(12):
            a, b, c, d = s, s - 1, s - 2, s - 3
            if 0 <= b < 8:
                std1(b)
            if 0 <= c < 8:
                leaky1(c, 0)
            if 0 <= b < 8:
                slope1(b)
            if 0 <= c < 8:
                leaky1(c, 1)
            if 0 <= b < 8:
                shift1(b)
            if 0 <= d < 8:
                store(d, 0)
                store(d, 1)
            if 0 <= b < 8:
                apply1(b, 0)
                apply1(b, 1)
            if a < 8:
                for h in range(2):
                    conv1(a, h, range(3, 4) if a < 4 else range(0, 4))
                bn1(a)
            if 0 <= c < 8:
                turn1(c, 0)
                turn1(c, 1)
